import numpy as np
import ml_dtypes


def mxq(x, axis, fmt="e4m3"):
    dtype, down = {"e4m3": (ml_dtypes.float8_e4m3fn, 7), "e5m2": (ml_dtypes.float8_e5m2, 14)}[fmt]
    v = np.moveaxis(np.asarray(x, np.float32).astype(ml_dtypes.bfloat16).astype(np.float64), axis, -1)
    blocks = v.reshape(v.shape[:-1] + (-1, 32))
    amax = np.abs(blocks).max(-1, keepdims=True)
    byte = np.maximum(np.where(amax > 0, np.frexp(amax)[1] - 1 + 127, 0) - down, 1)
    scale = np.exp2(byte - 127.0)
    codes = (blocks / scale).astype(np.float32).astype(dtype).astype(np.float64)
    return np.moveaxis((codes * scale).reshape(v.shape), -1, axis)


WIDE = False


def mx_kscale(k):
    if not WIDE:
        return np.ones(k)
    levels = np.array([10, -10, 5, -5, 0])
    a = np.random.permutation(np.resize(levels, k // 512 * 4)).reshape(k // 512, 4)
    idx = np.arange(k)
    return np.exp2(a[idx // 512, idx % 128 // 32])


BF16 = ml_dtypes.bfloat16


def bf(x):
    return np.asarray(x, np.float32).astype(BF16)


def f64(x):
    return np.asarray(x).astype(np.float64)


E2M1 = np.array([0.0, 0.5, 1.0, 1.5, 2.0, 3.0, 4.0, 6.0, -0.0, -0.5, -1.0, -1.5, -2.0, -3.0, -4.0, -6.0])


def pack_weight(w, fmt):
    k, n = w.shape
    w = f64(bf(w)).reshape(k // 32, 32, n)
    amax = np.abs(w).max(1)
    if fmt == "e4m3":
        byte = np.frexp(amax)[1] - 1 + 127 - 7
    else:
        mant, ex = np.frexp(amax / 6.0)
        byte = np.where(mant > 0.5, ex, ex - 1) + 127
    byte = np.clip(np.where(amax > 0, byte, 1), 1, 254)
    scaled = (w * np.exp2(127.0 - byte)[:, None, :]).reshape(k, n).astype(np.float32)
    by_word = np.ascontiguousarray(scaled.reshape(k // 512, 128, 4, n).transpose(0, 1, 3, 2))
    if fmt == "e4m3":
        words = by_word.astype(ml_dtypes.float8_e4m3fn).view(np.uint8)
    else:
        c = by_word.astype(ml_dtypes.float4_e2m1fn).view(np.uint8) & 0xF
        words = c[..., 0::2] | (c[..., 1::2] << 4)
    return np.ascontiguousarray(words), np.ascontiguousarray(byte.astype(np.uint8).reshape(k // 512, 16, n))


def unpack_weight(words, scales, fmt):
    g, p, n, _ = words.shape
    if fmt == "e4m3":
        vals = np.ascontiguousarray(words).view(ml_dtypes.float8_e4m3fn).astype(np.float64)
    else:
        nib = np.empty((g, p, n, 4), np.uint8)
        nib[..., 0::2] = words & 0xF
        nib[..., 1::2] = words >> 4
        vals = E2M1[nib]
    vals = vals * np.repeat(np.exp2(scales.astype(np.float64) - 127.0), 8, axis=1)[..., None]
    return vals.transpose(0, 1, 3, 2).reshape(g * 512, n)


B, I, H = 128, 15872, 512
FMT = "e4m3"


def sigmoid(v):
    return 1.0 / (1.0 + np.exp(-v))


def setup_inputs():
    s = mx_kscale(I + H)
    sx, sh = s[:I], s[I:]

    def wx():
        return pack_weight((np.random.standard_normal((H, I)) * 0.7 / np.sqrt(I) / sx).T, FMT)

    def wh():
        return pack_weight((np.random.standard_normal((H, H)) * 0.7 / np.sqrt(H) / sh).T, FMT)

    def bias():
        return bf(np.random.standard_normal(H) * 0.3)

    out = {}
    out["x"] = bf(np.random.standard_normal((B, I)) * sx)
    out["h"] = bf(np.random.standard_normal((B, H)) * sh)
    out["c"] = bf(np.random.standard_normal((B, H)))
    for name in ("weight_ii", "weight_if", "weight_ig", "weight_io"):
        words, scales = wx()
        out[name + "_words"] = words
        out[name + "_scales"] = scales
    for name in ("weight_hi", "weight_hf", "weight_hg", "weight_ho"):
        words, scales = wh()
        out[name + "_words"] = words
        out[name + "_scales"] = scales
    for name in ("bias_i", "bias_f", "bias_g", "bias_o"):
        out[name] = bias()
    return out


def reference(x, h, c,
              weight_ii_words, weight_ii_scales, weight_if_words, weight_if_scales,
              weight_ig_words, weight_ig_scales, weight_io_words, weight_io_scales,
              weight_hi_words, weight_hi_scales, weight_hf_words, weight_hf_scales,
              weight_hg_words, weight_hg_scales, weight_ho_words, weight_ho_scales,
              bias_i, bias_f, bias_g, bias_o):
    W_x = np.concatenate([unpack_weight(weight_ii_words, weight_ii_scales, FMT).T,
                          unpack_weight(weight_if_words, weight_if_scales, FMT).T,
                          unpack_weight(weight_ig_words, weight_ig_scales, FMT).T,
                          unpack_weight(weight_io_words, weight_io_scales, FMT).T], axis=0)
    W_h = np.concatenate([unpack_weight(weight_hi_words, weight_hi_scales, FMT).T,
                          unpack_weight(weight_hf_words, weight_hf_scales, FMT).T,
                          unpack_weight(weight_hg_words, weight_hg_scales, FMT).T,
                          unpack_weight(weight_ho_words, weight_ho_scales, FMT).T], axis=0)
    b = np.concatenate([f64(bias_i), f64(bias_f), f64(bias_g), f64(bias_o)], axis=0)
    z = np.concatenate([f64(x), f64(h)], axis=1)
    W = np.concatenate([W_x, W_h], axis=1)
    gates = (mxq(z, 1, "e4m3") @ W.T) + b
    gi, gf, gg, go = np.split(gates, 4, axis=1)
    i = sigmoid(gi)
    f = sigmoid(gf)
    g = np.tanh(gg)
    o = sigmoid(go)
    c_new = f * c_in(c) + i * g
    h_new = o * np.tanh(c_new)
    return (h_new, c_new)


def c_in(c):
    return f64(c)

@@ -1,0 +1,212 @@
+from contextlib import ExitStack
+
+import concourse.mybir as mybir
+from concourse.masks import make_identity
+
+FP8X4 = mybir.dt.float8_e4m3fn_x4
+BF16 = mybir.dt.bfloat16
+F32 = mybir.dt.float32
+I32 = mybir.dt.int32
+U32 = mybir.dt.uint32
+U8 = mybir.dt.uint8
+ACT = mybir.ActivationFunctionType
+ALU = mybir.AluOpType
+
+P = 128
+BATCH = 128
+IN_FEATURES = 15872
+HIDDEN = 512
+K_PASS = 4 * P
+X_PASSES = IN_FEATURES // K_PASS
+PASSES = X_PASSES + HIDDEN // K_PASS
+CHUNK = 4
+CHUNKS = PASSES // CHUNK
+LAST = CHUNKS - 1
+WORDS_PASS = K_PASS // 2
+QUADRANT = 32
+WEIGHT_BUFS = 12
+
+FLOPS = 2 * BATCH * (IN_FEATURES + HIDDEN) * 4 * HIDDEN
+
+
+def load_scale_planes(nc, planes, x_scales, h_scales):
+    for j in range(CHUNK):
+        own_passes = len(range(j, X_PASSES, CHUNK))
+        for r in range(4):
+            nc.gpsimd.dma_start(
+                out=planes[4 * j + r : P : QUADRANT, 0:own_passes, :].bitcast(F32),
+                in_=x_scales[j:X_PASSES:CHUNK, r:16:4, :].rearrange("q a n -> a q n").bitcast(F32),
+            )
+    for r in range(4):
+        nc.gpsimd.dma_start(
+            out=planes[4 * (CHUNK - 1) + r : P : QUADRANT, LAST, :].bitcast(F32),
+            in_=h_scales[0, r:16:4, :].bitcast(F32),
+        )
+
+
+def tile_forcedgpulstmcell_k_kernel(
+    tc,
+    x,
+    h,
+    c,
+    weight_ii_words,
+    weight_ii_scales,
+    weight_if_words,
+    weight_if_scales,
+    weight_ig_words,
+    weight_ig_scales,
+    weight_io_words,
+    weight_io_scales,
+    weight_hi_words,
+    weight_hi_scales,
+    weight_hf_words,
+    weight_hf_scales,
+    weight_hg_words,
+    weight_hg_scales,
+    weight_ho_words,
+    weight_ho_scales,
+    bias_i,
+    bias_f,
+    bias_g,
+    bias_o,
+    h_new,
+    c_new,
+):
+    nc = tc.nc
+    x_words = [weight_ii_words, weight_if_words, weight_ig_words, weight_io_words]
+    x_scales = [weight_ii_scales, weight_if_scales, weight_ig_scales, weight_io_scales]
+    h_words = [weight_hi_words, weight_hf_words, weight_hg_words, weight_ho_words]
+    h_scales = [weight_hi_scales, weight_hf_scales, weight_hg_scales, weight_ho_scales]
+    biases = [bias_i, bias_f, bias_g, bias_o]
+    GATES = len(biases)
+
+    with ExitStack() as stack:
+        stack.enter_context(tc.manual_schedule())
+        keep = stack.enter_context(tc.tile_pool(name="keep", bufs=1))
+        raw_pool = stack.enter_context(tc.tile_pool(name="raw", bufs=CHUNKS))
+        stage = stack.enter_context(tc.tile_pool(name="stage", bufs=3))
+        weights = stack.enter_context(tc.tile_pool(name="weights", bufs=WEIGHT_BUFS))
+        psum_t = stack.enter_context(tc.psum_pool(name="psum_t", bufs=4))
+        psum_bias = stack.enter_context(tc.psum_pool(name="psum_bias", bufs=2))
+        psum_acc = stack.enter_context(tc.psum_pool(name="psum_acc", bufs=2))
+
+        raws = []
+        for q in range(CHUNKS):
+            raw = raw_pool.tile([P, CHUNK * K_PASS], BF16, name="raw")
+            first = q * CHUNK * K_PASS
+            if q < LAST:
+                nc.sync.dma_start(out=raw[:], in_=x[:, first : first + CHUNK * K_PASS])
+            else:
+                nc.sync.dma_start(out=raw[:, : IN_FEATURES - first], in_=x[:, first:])
+                nc.sync.dma_start(out=raw[:, IN_FEATURES - first :], in_=h)
+            raws.append(raw)
+        c_sb = keep.tile([P, HIDDEN], BF16, name="c_sb")
+        nc.sync.dma_start(out=c_sb[:], in_=c)
+
+        planes = []
+        for n in range(GATES):
+            gate_planes = keep.tile([P, CHUNKS, HIDDEN], U8, align_bytes=64, name="planes%d" % n)
+            nc.vector.memset(gate_planes[:].bitcast(I32), 0)
+            planes.append(gate_planes)
+        ident = keep.tile([P, P], F32, name="ident")
+        make_identity(nc, ident[:])
+        for n in range(GATES):
+            load_scale_planes(nc, planes[n], x_scales[n], h_scales[n])
+
+        bias_rows = keep.tile([P, GATES * HIDDEN], BF16, name="bias_rows")
+        nc.vector.memset(bias_rows[:], 0.0)
+        ones = keep.tile([P, P], BF16, name="ones")
+        nc.vector.memset(ones[:], 1.0)
+        for n in range(GATES):
+            nc.scalar.dma_start(
+                out=bias_rows[0:1, n * HIDDEN : (n + 1) * HIDDEN],
+                in_=biases[n].rearrange("(o n) -> o n", o=1),
+            )
+
+        x_codes = keep.tile([P, PASSES * BATCH], U32, align_bytes=64, name="x_codes")
+        x_planes = keep.tile([P, PASSES * BATCH], U8, align_bytes=64, name="x_planes")
+        for q in range(CHUNKS):
+            raw_words = raws[q][:].bitcast(F32)
+            grouped = stage.tile([P, CHUNK * K_PASS], BF16, align_bytes=64, name="grouped")
+            grouped_words = grouped[:].bitcast(F32).rearrange("p (g b u) -> p g b u", g=CHUNK, u=2)
+            for half in range(2):
+                xt = psum_t.tile([P, 2, 2, BATCH], F32, name="xt")
+                for g in range(2):
+                    first = (2 * half + g) * WORDS_PASS
+                    for u in range(2):
+                        nc.tensor.transpose(
+                            xt[:, g, u, :], raw_words[:, first + u : first + WORDS_PASS : 2], ident[:]
+                        )
+                side_by_side = xt[:].rearrange("p g u b -> p g b u")
+                if half == 0:
+                    nc.vector.tensor_copy(out=grouped_words[:, 0:2], in_=side_by_side)
+                else:
+                    nc.scalar.copy(out=grouped_words[:, 2:4], in_=side_by_side)
+            cols = slice(q * CHUNK * BATCH, (q + 1) * CHUNK * BATCH)
+            nc.vector.quantize_mx(
+                out=x_codes[:, cols].bitcast(FP8X4), scales=x_planes[:, cols], in_=grouped[:]
+            )
+
+        bias_all = keep.tile([P, GATES, HIDDEN], F32, name="bias_all")
+        for n in range(GATES):
+            spread = psum_bias.tile([P, HIDDEN], F32, name="spread")
+            nc.tensor.matmul(
+                out=spread[:],
+                lhsT=ones[:],
+                rhs=bias_rows[:, n * HIDDEN : (n + 1) * HIDDEN],
+                start=True,
+                stop=True,
+            )
+            nc.scalar.copy(out=bias_all[:, n, :], in_=spread[:])
+
+        def gate(n, func):
+            acc = psum_acc.tile([P, HIDDEN], F32, name="acc")
+            for q in range(CHUNKS):
+                w = weights.tile([P, CHUNK, HIDDEN], U32, align_bytes=64, name="w")
+                from_x = min(CHUNK, X_PASSES - q * CHUNK)
+                nc.sync.dma_start(
+                    out=w[:, 0:from_x, :].bitcast(I32),
+                    in_=x_words[n][q * CHUNK : q * CHUNK + from_x]
+                    .rearrange("g p n t -> p g (n t)")
+                    .bitcast(I32),
+                )
+                if from_x < CHUNK:
+                    nc.sync.dma_start(
+                        out=w[:, from_x, :].bitcast(I32),
+                        in_=h_words[n][0].rearrange("p n t -> p (n t)").bitcast(I32),
+                    )
+                for j in range(CHUNK):
+                    g = q * CHUNK + j
+                    nc.tensor.matmul_mx(
+                        out=acc[:],
+                        lhsT=x_codes[:, g * BATCH : (g + 1) * BATCH].bitcast(FP8X4),
+                        lhsT_scale=x_planes[:, g * BATCH : (g + 1) * BATCH],
+                        rhs=w[:, j, :].bitcast(FP8X4),
+                        rhs_scale=planes[n][4 * j : P, q, :],
+                        start=(g == 0),
+                        stop=(g == PASSES - 1),
+                    )
+            biased = stage.tile([P, HIDDEN], F32, name="biased")
+            nc.vector.tensor_tensor(out=biased[:], in0=acc[:], in1=bias_all[:, n, :], op=ALU.add)
+            result = keep.tile([P, HIDDEN], F32, name="gate%d" % n)
+            nc.scalar.activation(out=result[:], in_=biased[:], func=func)
+            return result
+
+        i_gate = gate(0, ACT.Sigmoid)
+        f_gate = gate(1, ACT.Sigmoid)
+        kept = keep.tile([P, HIDDEN], F32, name="kept")
+        nc.vector.tensor_mul(out=kept[:], in0=f_gate[:], in1=c_sb[:])
+
+        g_gate = gate(2, ACT.Tanh)
+        fresh = keep.tile([P, HIDDEN], F32, name="fresh")
+        nc.vector.tensor_mul(out=fresh[:], in0=i_gate[:], in1=g_gate[:])
+        c_out = keep.tile([P, HIDDEN], F32, name="c_out")
+        nc.vector.tensor_add(out=c_out[:], in0=kept[:], in1=fresh[:])
+        nc.scalar.dma_start(out=c_new, in_=c_out[:])
+        tanh_c = keep.tile([P, HIDDEN], F32, name="tanh_c")
+        nc.scalar.activation(out=tanh_c[:], in_=c_out[:], func=ACT.Tanh)
+
+        o_gate = gate(3, ACT.Sigmoid)
+        h_out = keep.tile([P, HIDDEN], F32, name="h_out")
+        nc.vector.tensor_mul(out=h_out[:], in0=o_gate[:], in1=tanh_c[:])
+        nc.sync.dma_start(out=h_new, in_=h_out[:])

@@ -29,19 +29,20 @@ WEIGHT_BUFS = 12
 FLOPS = 2 * BATCH * (IN_FEATURES + HIDDEN) * 4 * HIDDEN
 
 
-def load_scale_planes(nc, planes, x_scales, h_scales):
+def scale_rows(planes, x_scales, h_scales):
+    rows = []
     for j in range(CHUNK):
         own_passes = len(range(j, X_PASSES, CHUNK))
         for r in range(4):
-            nc.gpsimd.dma_start(
-                out=planes[4 * j + r : P : QUADRANT, 0:own_passes, :].bitcast(F32),
-                in_=x_scales[j:X_PASSES:CHUNK, r:16:4, :].rearrange("q a n -> a q n").bitcast(F32),
+            rows.append(
+                (
+                    planes[4 * j + r : P : QUADRANT, 0:own_passes, :],
+                    x_scales[j:X_PASSES:CHUNK, r:16:4, :].rearrange("q a n -> a q n"),
+                )
             )
     for r in range(4):
-        nc.gpsimd.dma_start(
-            out=planes[4 * (CHUNK - 1) + r : P : QUADRANT, LAST, :].bitcast(F32),
-            in_=h_scales[0, r:16:4, :].bitcast(F32),
-        )
+        rows.append((planes[4 * (CHUNK - 1) + r : P : QUADRANT, LAST, :], h_scales[0, r:16:4, :]))
+    return rows
 
 
 def tile_forcedgpulstmcell_k_kernel(
@@ -90,28 +91,37 @@ def tile_forcedgpulstmcell_k_kernel(
         psum_bias = stack.enter_context(tc.psum_pool(name="psum_bias", bufs=2))
         psum_acc = stack.enter_context(tc.psum_pool(name="psum_acc", bufs=2))
 
-        raws = []
-        for q in range(CHUNKS):
-            raw = raw_pool.tile([P, CHUNK * K_PASS], BF16, name="raw")
-            first = q * CHUNK * K_PASS
-            if q < LAST:
-                nc.sync.dma_start(out=raw[:], in_=x[:, first : first + CHUNK * K_PASS])
-            else:
-                nc.sync.dma_start(out=raw[:, : IN_FEATURES - first], in_=x[:, first:])
-                nc.sync.dma_start(out=raw[:, IN_FEATURES - first :], in_=h)
-            raws.append(raw)
-        c_sb = keep.tile([P, HIDDEN], BF16, name="c_sb")
-        nc.sync.dma_start(out=c_sb[:], in_=c)
-
         planes = []
         for n in range(GATES):
             gate_planes = keep.tile([P, CHUNKS, HIDDEN], U8, align_bytes=64, name="planes%d" % n)
             nc.vector.memset(gate_planes[:].bitcast(I32), 0)
             planes.append(gate_planes)
+
+        early = []
+        raws = []
+        for q in range(CHUNKS):
+            raw = raw_pool.tile([P, CHUNK * K_PASS], BF16, name="raw")
+            first = q * CHUNK * K_PASS
+            if q < LAST:
+                early.append((raw[:], x[:, first : first + CHUNK * K_PASS]))
+            else:
+                early.append((raw[:, : IN_FEATURES - first], x[:, first:]))
+                early.append((raw[:, IN_FEATURES - first :], h))
+            raws.append(raw)
+        c_sb = keep.tile([P, HIDDEN], BF16, name="c_sb")
+        early.append((c_sb[:], c))
+        first_rows = scale_rows(planes[0], x_scales[0], h_scales[0])
+        share = len(first_rows) // len(early)
+        for k, (dst, src) in enumerate(early):
+            nc.sync.dma_start(out=dst, in_=src)
+            for dst_rows, src_rows in first_rows[k * share : (k + 1) * share]:
+                nc.sync.dma_start(out=dst_rows.bitcast(I32), in_=src_rows.bitcast(I32))
+
         ident = keep.tile([P, P], F32, name="ident")
         make_identity(nc, ident[:])
-        for n in range(GATES):
-            load_scale_planes(nc, planes[n], x_scales[n], h_scales[n])
+        for n in range(1, GATES):
+            for dst_rows, src_rows in scale_rows(planes[n], x_scales[n], h_scales[n]):
+                nc.gpsimd.dma_start(out=dst_rows.bitcast(F32), in_=src_rows.bitcast(F32))
 
         bias_rows = keep.tile([P, GATES * HIDDEN], BF16, name="bias_rows")
         nc.vector.memset(bias_rows[:], 0.0)

@@ -24,25 +24,21 @@ CHUNKS = PASSES // CHUNK
 LAST = CHUNKS - 1
 WORDS_PASS = K_PASS // 2
 QUADRANT = 32
-WEIGHT_BUFS = 12
+WEIGHT_BUFS = 8
 
 FLOPS = 2 * BATCH * (IN_FEATURES + HIDDEN) * 4 * HIDDEN
 
 
-def scale_rows(planes, x_scales, h_scales):
-    rows = []
-    for j in range(CHUNK):
-        own_passes = len(range(j, X_PASSES, CHUNK))
-        for r in range(4):
-            rows.append(
-                (
-                    planes[4 * j + r : P : QUADRANT, 0:own_passes, :],
-                    x_scales[j:X_PASSES:CHUNK, r:16:4, :].rearrange("q a n -> a q n"),
-                )
-            )
+def load_scale_planes(nc, planes, first, x_scales, h_scales):
     for r in range(4):
-        rows.append((planes[4 * (CHUNK - 1) + r : P : QUADRANT, LAST, :], h_scales[0, r:16:4, :]))
-    return rows
+        rows = planes[first + r : P : QUADRANT]
+        nc.gpsimd.dma_start(
+            out=rows[:, 0:X_PASSES, :].bitcast(F32),
+            in_=x_scales[:, r:16:4, :].rearrange("g a n -> a g n").bitcast(F32),
+        )
+        nc.gpsimd.dma_start(
+            out=rows[:, X_PASSES, :].bitcast(F32), in_=h_scales[0, r:16:4, :].bitcast(F32)
+        )
 
 
 def tile_forcedgpulstmcell_k_kernel(
@@ -85,43 +81,33 @@ def tile_forcedgpulstmcell_k_kernel(
         stack.enter_context(tc.manual_schedule())
         keep = stack.enter_context(tc.tile_pool(name="keep", bufs=1))
         raw_pool = stack.enter_context(tc.tile_pool(name="raw", bufs=CHUNKS))
-        stage = stack.enter_context(tc.tile_pool(name="stage", bufs=3))
+        stage = stack.enter_context(tc.tile_pool(name="stage", bufs=2))
         weights = stack.enter_context(tc.tile_pool(name="weights", bufs=WEIGHT_BUFS))
         psum_t = stack.enter_context(tc.psum_pool(name="psum_t", bufs=4))
         psum_bias = stack.enter_context(tc.psum_pool(name="psum_bias", bufs=2))
         psum_acc = stack.enter_context(tc.psum_pool(name="psum_acc", bufs=2))
 
-        planes = []
-        for n in range(GATES):
-            gate_planes = keep.tile([P, CHUNKS, HIDDEN], U8, align_bytes=64, name="planes%d" % n)
-            nc.vector.memset(gate_planes[:].bitcast(I32), 0)
-            planes.append(gate_planes)
-
-        early = []
         raws = []
         for q in range(CHUNKS):
             raw = raw_pool.tile([P, CHUNK * K_PASS], BF16, name="raw")
             first = q * CHUNK * K_PASS
             if q < LAST:
-                early.append((raw[:], x[:, first : first + CHUNK * K_PASS]))
+                nc.sync.dma_start(out=raw[:], in_=x[:, first : first + CHUNK * K_PASS])
             else:
-                early.append((raw[:, : IN_FEATURES - first], x[:, first:]))
-                early.append((raw[:, IN_FEATURES - first :], h))
+                nc.sync.dma_start(out=raw[:, : IN_FEATURES - first], in_=x[:, first:])
+                nc.sync.dma_start(out=raw[:, IN_FEATURES - first :], in_=h)
             raws.append(raw)
         c_sb = keep.tile([P, HIDDEN], BF16, name="c_sb")
-        early.append((c_sb[:], c))
-        first_rows = scale_rows(planes[0], x_scales[0], h_scales[0])
-        share = len(first_rows) // len(early)
-        for k, (dst, src) in enumerate(early):
-            nc.sync.dma_start(out=dst, in_=src)
-            for dst_rows, src_rows in first_rows[k * share : (k + 1) * share]:
-                nc.sync.dma_start(out=dst_rows.bitcast(I32), in_=src_rows.bitcast(I32))
+        nc.sync.dma_start(out=c_sb[:], in_=c)
 
         ident = keep.tile([P, P], F32, name="ident")
         make_identity(nc, ident[:])
-        for n in range(1, GATES):
-            for dst_rows, src_rows in scale_rows(planes[n], x_scales[n], h_scales[n]):
-                nc.gpsimd.dma_start(out=dst_rows.bitcast(F32), in_=src_rows.bitcast(F32))
+        planes = []
+        for n in range(GATES):
+            gate_planes = keep.tile([P, PASSES, HIDDEN], U8, align_bytes=64, name="planes%d" % n)
+            nc.vector.memset(gate_planes[:].bitcast(I32), 0)
+            load_scale_planes(nc, gate_planes, 4 * n, x_scales[n], h_scales[n])
+            planes.append(gate_planes)
 
         bias_rows = keep.tile([P, GATES * HIDDEN], BF16, name="bias_rows")
         nc.vector.memset(bias_rows[:], 0.0)
@@ -192,7 +178,7 @@ def tile_forcedgpulstmcell_k_kernel(
                         lhsT=x_codes[:, g * BATCH : (g + 1) * BATCH].bitcast(FP8X4),
                         lhsT_scale=x_planes[:, g * BATCH : (g + 1) * BATCH],
                         rhs=w[:, j, :].bitcast(FP8X4),
-                        rhs_scale=planes[n][4 * j : P, q, :],
+                        rhs_scale=planes[n][4 * n : P, g, :],
                         start=(g == 0),
                         stop=(g == PASSES - 1),
                     )

@@ -24,21 +24,30 @@ CHUNKS = PASSES // CHUNK
 LAST = CHUNKS - 1
 WORDS_PASS = K_PASS // 2
 QUADRANT = 32
-WEIGHT_BUFS = 8
+WEIGHT_BUFS = 12
 
 FLOPS = 2 * BATCH * (IN_FEATURES + HIDDEN) * 4 * HIDDEN
 
 
-def load_scale_planes(nc, planes, first, x_scales, h_scales):
-    for r in range(4):
-        rows = planes[first + r : P : QUADRANT]
-        nc.gpsimd.dma_start(
-            out=rows[:, 0:X_PASSES, :].bitcast(F32),
-            in_=x_scales[:, r:16:4, :].rearrange("g a n -> a g n").bitcast(F32),
+def scale_loads(planes, x_scales, h_scales):
+    whole = X_PASSES // CHUNK
+    rest = X_PASSES - whole * CHUNK
+    whole_chunks = []
+    last_chunk = []
+    for a in range(4):
+        live = planes[QUADRANT * a : QUADRANT * a + 4 * CHUNK]
+        for r in range(4):
+            whole_chunks.append(
+                (
+                    live[r : 4 * CHUNK : 4, 0:whole, :],
+                    x_scales[0 : whole * CHUNK, 4 * a + r, :].rearrange("(q j) n -> j q n", j=CHUNK),
+                )
+            )
+        last_chunk.append(
+            (live[0 : 4 * rest, LAST, :], x_scales[whole * CHUNK : X_PASSES, 4 * a : 4 * a + 4, :])
         )
-        nc.gpsimd.dma_start(
-            out=rows[:, X_PASSES, :].bitcast(F32), in_=h_scales[0, r:16:4, :].bitcast(F32)
-        )
+        last_chunk.append((live[4 * rest : 4 * CHUNK, LAST, :], h_scales[0, 4 * a : 4 * a + 4, :]))
+    return whole_chunks, last_chunk
 
 
 def tile_forcedgpulstmcell_k_kernel(
@@ -81,11 +90,28 @@ def tile_forcedgpulstmcell_k_kernel(
         stack.enter_context(tc.manual_schedule())
         keep = stack.enter_context(tc.tile_pool(name="keep", bufs=1))
         raw_pool = stack.enter_context(tc.tile_pool(name="raw", bufs=CHUNKS))
-        stage = stack.enter_context(tc.tile_pool(name="stage", bufs=2))
+        stage = stack.enter_context(tc.tile_pool(name="stage", bufs=3))
         weights = stack.enter_context(tc.tile_pool(name="weights", bufs=WEIGHT_BUFS))
         psum_t = stack.enter_context(tc.psum_pool(name="psum_t", bufs=4))
         psum_bias = stack.enter_context(tc.psum_pool(name="psum_bias", bufs=2))
         psum_acc = stack.enter_context(tc.psum_pool(name="psum_acc", bufs=2))
+
+        planes = []
+        small_loads = []
+        ident = keep.tile([P, P], F32, name="ident")
+        make_identity(nc, ident[:])
+        for n in range(GATES):
+            gate_planes = keep.tile([P, CHUNKS, HIDDEN], U8, align_bytes=64, name="planes%d" % n)
+            nc.vector.memset(gate_planes[:].bitcast(I32), 0)
+            planes.append(gate_planes)
+            whole_chunks, last_chunk = scale_loads(gate_planes, x_scales[n], h_scales[n])
+            small_loads.append(last_chunk)
+            for dst, src in whole_chunks:
+                nc.gpsimd.dma_start(out=dst.bitcast(F32), in_=src.bitcast(F32))
+
+        def small_load(n, k):
+            dst, src = small_loads[n][k]
+            nc.sync.dma_start(out=dst.bitcast(I32), in_=src.bitcast(I32))
 
         raws = []
         for q in range(CHUNKS):
@@ -96,18 +122,10 @@ def tile_forcedgpulstmcell_k_kernel(
             else:
                 nc.sync.dma_start(out=raw[:, : IN_FEATURES - first], in_=x[:, first:])
                 nc.sync.dma_start(out=raw[:, IN_FEATURES - first :], in_=h)
+            small_load(0, q)
             raws.append(raw)
         c_sb = keep.tile([P, HIDDEN], BF16, name="c_sb")
         nc.sync.dma_start(out=c_sb[:], in_=c)
-
-        ident = keep.tile([P, P], F32, name="ident")
-        make_identity(nc, ident[:])
-        planes = []
-        for n in range(GATES):
-            gate_planes = keep.tile([P, PASSES, HIDDEN], U8, align_bytes=64, name="planes%d" % n)
-            nc.vector.memset(gate_planes[:].bitcast(I32), 0)
-            load_scale_planes(nc, gate_planes, 4 * n, x_scales[n], h_scales[n])
-            planes.append(gate_planes)
 
         bias_rows = keep.tile([P, GATES * HIDDEN], BF16, name="bias_rows")
         nc.vector.memset(bias_rows[:], 0.0)
@@ -171,6 +189,8 @@ def tile_forcedgpulstmcell_k_kernel(
                         out=w[:, from_x, :].bitcast(I32),
                         in_=h_words[n][0].rearrange("p n t -> p (n t)").bitcast(I32),
                     )
+                if n + 1 < GATES:
+                    small_load(n + 1, q)
                 for j in range(CHUNK):
                     g = q * CHUNK + j
                     nc.tensor.matmul_mx(
@@ -178,7 +198,7 @@ def tile_forcedgpulstmcell_k_kernel(
                         lhsT=x_codes[:, g * BATCH : (g + 1) * BATCH].bitcast(FP8X4),
                         lhsT_scale=x_planes[:, g * BATCH : (g + 1) * BATCH],
                         rhs=w[:, j, :].bitcast(FP8X4),
-                        rhs_scale=planes[n][4 * n : P, g, :],
+                        rhs_scale=planes[n][4 * j : P, q, :],
                         start=(g == 0),
                         stop=(g == PASSES - 1),
                     )

@@ -93,8 +93,8 @@ def tile_forcedgpulstmcell_k_kernel(
         stage = stack.enter_context(tc.tile_pool(name="stage", bufs=3))
         weights = stack.enter_context(tc.tile_pool(name="weights", bufs=WEIGHT_BUFS))
         psum_t = stack.enter_context(tc.psum_pool(name="psum_t", bufs=4))
-        psum_bias = stack.enter_context(tc.psum_pool(name="psum_bias", bufs=2))
-        psum_acc = stack.enter_context(tc.psum_pool(name="psum_acc", bufs=2))
+        psum_bias = stack.enter_context(tc.psum_pool(name="psum_bias", bufs=1))
+        psum_acc = stack.enter_context(tc.psum_pool(name="psum_acc", bufs=3))
 
         planes = []
         small_loads = []
@@ -173,8 +173,12 @@ def tile_forcedgpulstmcell_k_kernel(
             )
             nc.scalar.copy(out=bias_all[:, n, :], in_=spread[:])
 
-        def gate(n, func):
-            acc = psum_acc.tile([P, HIDDEN], F32, name="acc")
+        def gate(n, func, parts):
+            width = HIDDEN // parts
+            accs = []
+            for part in range(parts):
+                acc = psum_acc.tile([P, HIDDEN], F32, name="acc")
+                accs.append(acc)
             for q in range(CHUNKS):
                 w = weights.tile([P, CHUNK, HIDDEN], U32, align_bytes=64, name="w")
                 from_x = min(CHUNK, X_PASSES - q * CHUNK)
@@ -193,27 +197,40 @@ def tile_forcedgpulstmcell_k_kernel(
                     small_load(n + 1, q)
                 for j in range(CHUNK):
                     g = q * CHUNK + j
-                    nc.tensor.matmul_mx(
-                        out=acc[:],
-                        lhsT=x_codes[:, g * BATCH : (g + 1) * BATCH].bitcast(FP8X4),
-                        lhsT_scale=x_planes[:, g * BATCH : (g + 1) * BATCH],
-                        rhs=w[:, j, :].bitcast(FP8X4),
-                        rhs_scale=planes[n][4 * j : P, q, :],
-                        start=(g == 0),
-                        stop=(g == PASSES - 1),
-                    )
-            biased = stage.tile([P, HIDDEN], F32, name="biased")
-            nc.vector.tensor_tensor(out=biased[:], in0=acc[:], in1=bias_all[:, n, :], op=ALU.add)
-            result = keep.tile([P, HIDDEN], F32, name="gate%d" % n)
-            nc.scalar.activation(out=result[:], in_=biased[:], func=func)
-            return result
+                    for part in range(parts):
+                        cols = slice(part * width, (part + 1) * width)
+                        nc.tensor.matmul_mx(
+                            out=accs[part][:, 0:width],
+                            lhsT=x_codes[:, g * BATCH : (g + 1) * BATCH].bitcast(FP8X4),
+                            lhsT_scale=x_planes[:, g * BATCH : (g + 1) * BATCH],
+                            rhs=w[:, j, cols].bitcast(FP8X4),
+                            rhs_scale=planes[n][4 * j : P, q, cols],
+                            start=(g == 0),
+                            stop=(g == PASSES - 1),
+                        )
+            biased = []
+            for part in range(parts):
+                total = stage.tile([P, HIDDEN], F32, name="total")
+                nc.vector.tensor_tensor(
+                    out=total[:, 0:width],
+                    in0=accs[part][:, 0:width],
+                    in1=bias_all[:, n, part * width : (part + 1) * width],
+                    op=ALU.add,
+                )
+                biased.append(total)
+            results = []
+            for part in range(parts):
+                result = keep.tile([P, width], F32, name="gate%d_%d" % (n, part))
+                nc.scalar.activation(out=result[:], in_=biased[part][:, 0:width], func=func)
+                results.append(result)
+            return results
 
-        i_gate = gate(0, ACT.Sigmoid)
-        f_gate = gate(1, ACT.Sigmoid)
+        (i_gate,) = gate(0, ACT.Sigmoid, 1)
+        (f_gate,) = gate(1, ACT.Sigmoid, 1)
         kept = keep.tile([P, HIDDEN], F32, name="kept")
         nc.vector.tensor_mul(out=kept[:], in0=f_gate[:], in1=c_sb[:])
 
-        g_gate = gate(2, ACT.Tanh)
+        (g_gate,) = gate(2, ACT.Tanh, 1)
         fresh = keep.tile([P, HIDDEN], F32, name="fresh")
         nc.vector.tensor_mul(out=fresh[:], in0=i_gate[:], in1=g_gate[:])
         c_out = keep.tile([P, HIDDEN], F32, name="c_out")
@@ -222,7 +239,10 @@ def tile_forcedgpulstmcell_k_kernel(
         tanh_c = keep.tile([P, HIDDEN], F32, name="tanh_c")
         nc.scalar.activation(out=tanh_c[:], in_=c_out[:], func=ACT.Tanh)
 
-        o_gate = gate(3, ACT.Sigmoid)
-        h_out = keep.tile([P, HIDDEN], F32, name="h_out")
-        nc.vector.tensor_mul(out=h_out[:], in0=o_gate[:], in1=tanh_c[:])
-        nc.sync.dma_start(out=h_new, in_=h_out[:])
+        halves = gate(3, ACT.Sigmoid, 2)
+        width = HIDDEN // 2
+        for part, queue in ((0, nc.sync), (1, nc.scalar)):
+            cols = slice(part * width, (part + 1) * width)
+            h_out = keep.tile([P, width], F32, name="h_out%d" % part)
+            nc.vector.tensor_mul(out=h_out[:], in0=halves[part][:], in1=tanh_c[:, cols])
+            queue.dma_start(out=h_new[:, cols], in_=h_out[:])

@@ -34,15 +34,17 @@ def scale_loads(planes, x_scales, h_scales):
     rest = X_PASSES - whole * CHUNK
     whole_chunks = []
     last_chunk = []
-    for a in range(4):
-        live = planes[QUADRANT * a : QUADRANT * a + 4 * CHUNK]
-        for r in range(4):
+    for r in range(4):
+        for a in range(4):
+            live = planes[QUADRANT * a : QUADRANT * a + 4 * CHUNK]
             whole_chunks.append(
                 (
                     live[r : 4 * CHUNK : 4, 0:whole, :],
                     x_scales[0 : whole * CHUNK, 4 * a + r, :].rearrange("(q j) n -> j q n", j=CHUNK),
                 )
             )
+    for a in range(4):
+        live = planes[QUADRANT * a : QUADRANT * a + 4 * CHUNK]
         last_chunk.append(
             (live[0 : 4 * rest, LAST, :], x_scales[whole * CHUNK : X_PASSES, 4 * a : 4 * a + 4, :])
         )

@@ -21,6 +21,8 @@ X_PASSES = IN_FEATURES // K_PASS
 PASSES = X_PASSES + HIDDEN // K_PASS
 CHUNK = 4
 CHUNKS = PASSES // CHUNK
+WHOLE = X_PASSES // CHUNK
+SLOTS = WHOLE + 2
 LAST = CHUNKS - 1
 WORDS_PASS = K_PASS // 2
 QUADRANT = 32
@@ -30,26 +32,30 @@ FLOPS = 2 * BATCH * (IN_FEATURES + HIDDEN) * 4 * HIDDEN
 
 
 def scale_loads(planes, x_scales, h_scales):
-    whole = X_PASSES // CHUNK
-    rest = X_PASSES - whole * CHUNK
-    whole_chunks = []
-    last_chunk = []
+    of_x = []
+    of_h = []
     for r in range(4):
         for a in range(4):
             live = planes[QUADRANT * a : QUADRANT * a + 4 * CHUNK]
-            whole_chunks.append(
+            of_x.append(
                 (
-                    live[r : 4 * CHUNK : 4, 0:whole, :],
-                    x_scales[0 : whole * CHUNK, 4 * a + r, :].rearrange("(q j) n -> j q n", j=CHUNK),
+                    live[r : 4 * CHUNK : 4, 0:WHOLE, :],
+                    x_scales[0 : WHOLE * CHUNK, 4 * a + r, :].rearrange("(q j) n -> j q n", j=CHUNK),
                 )
             )
     for a in range(4):
         live = planes[QUADRANT * a : QUADRANT * a + 4 * CHUNK]
-        last_chunk.append(
-            (live[0 : 4 * rest, LAST, :], x_scales[whole * CHUNK : X_PASSES, 4 * a : 4 * a + 4, :])
-        )
-        last_chunk.append((live[4 * rest : 4 * CHUNK, LAST, :], h_scales[0, 4 * a : 4 * a + 4, :]))
-    return whole_chunks, last_chunk
+        of_x.append((live[:, WHOLE, :], x_scales[X_PASSES - CHUNK : X_PASSES, 4 * a : 4 * a + 4, :]))
+        of_h.append((live[0:4, WHOLE + 1, :], h_scales[0, 4 * a : 4 * a + 4, :]))
+    return of_x, of_h
+
+
+def plane_of(g):
+    if g < WHOLE * CHUNK:
+        return g % CHUNK, g // CHUNK
+    if g < X_PASSES:
+        return g - (X_PASSES - CHUNK), WHOLE
+    return 0, WHOLE + 1
 
 
 def tile_forcedgpulstmcell_k_kernel(
@@ -91,7 +97,7 @@ def tile_forcedgpulstmcell_k_kernel(
     with ExitStack() as stack:
         stack.enter_context(tc.manual_schedule())
         keep = stack.enter_context(tc.tile_pool(name="keep", bufs=1))
-        raw_pool = stack.enter_context(tc.tile_pool(name="raw", bufs=CHUNKS))
+        raw_pool = stack.enter_context(tc.tile_pool(name="raw", bufs=CHUNKS // 2))
         stage = stack.enter_context(tc.tile_pool(name="stage", bufs=3))
         weights = stack.enter_context(tc.tile_pool(name="weights", bufs=WEIGHT_BUFS))
         psum_t = stack.enter_context(tc.psum_pool(name="psum_t", bufs=4))
@@ -103,27 +109,28 @@ def tile_forcedgpulstmcell_k_kernel(
         ident = keep.tile([P, P], F32, name="ident")
         make_identity(nc, ident[:])
         for n in range(GATES):
-            gate_planes = keep.tile([P, CHUNKS, HIDDEN], U8, align_bytes=64, name="planes%d" % n)
+            gate_planes = keep.tile([P, SLOTS, HIDDEN], U8, align_bytes=64, name="planes%d" % n)
             nc.vector.memset(gate_planes[:].bitcast(I32), 0)
             planes.append(gate_planes)
-            whole_chunks, last_chunk = scale_loads(gate_planes, x_scales[n], h_scales[n])
-            small_loads.append(last_chunk)
-            for dst, src in whole_chunks:
+            of_x, of_h = scale_loads(gate_planes, x_scales[n], h_scales[n])
+            small_loads.append(of_h)
+            for dst, src in of_x:
                 nc.gpsimd.dma_start(out=dst.bitcast(F32), in_=src.bitcast(F32))
 
         def small_load(n, k):
-            dst, src = small_loads[n][k]
-            nc.sync.dma_start(out=dst.bitcast(I32), in_=src.bitcast(I32))
+            if n < GATES and k < len(small_loads[n]):
+                dst, src = small_loads[n][k]
+                nc.sync.dma_start(out=dst.bitcast(I32), in_=src.bitcast(I32))
 
         raws = []
-        for q in range(CHUNKS):
-            raw = raw_pool.tile([P, CHUNK * K_PASS], BF16, name="raw")
-            first = q * CHUNK * K_PASS
-            if q < LAST:
-                nc.sync.dma_start(out=raw[:], in_=x[:, first : first + CHUNK * K_PASS])
-            else:
-                nc.sync.dma_start(out=raw[:, : IN_FEATURES - first], in_=x[:, first:])
-                nc.sync.dma_start(out=raw[:, IN_FEATURES - first :], in_=h)
+        width = 2 * CHUNK * K_PASS
+        for q in range(CHUNKS // 2):
+            raw = raw_pool.tile([P, width], BF16, name="raw")
+            first = q * width
+            own = min(width, IN_FEATURES - first)
+            nc.sync.dma_start(out=raw[:, :own], in_=x[:, first : first + own])
+            if own < width:
+                nc.sync.dma_start(out=raw[:, own:], in_=h)
             small_load(0, q)
             raws.append(raw)
         c_sb = keep.tile([P, HIDDEN], BF16, name="c_sb")
@@ -142,7 +149,8 @@ def tile_forcedgpulstmcell_k_kernel(
         x_codes = keep.tile([P, PASSES * BATCH], U32, align_bytes=64, name="x_codes")
         x_planes = keep.tile([P, PASSES * BATCH], U8, align_bytes=64, name="x_planes")
         for q in range(CHUNKS):
-            raw_words = raws[q][:].bitcast(F32)
+            half_raw = CHUNK * K_PASS * (q % 2)
+            raw_words = raws[q // 2][:, half_raw : half_raw + CHUNK * K_PASS].bitcast(F32)
             grouped = stage.tile([P, CHUNK * K_PASS], BF16, align_bytes=64, name="grouped")
             grouped_words = grouped[:].bitcast(F32).rearrange("p (g b u) -> p g b u", g=CHUNK, u=2)
             for half in range(2):
@@ -195,10 +203,10 @@ def tile_forcedgpulstmcell_k_kernel(
                         out=w[:, from_x, :].bitcast(I32),
                         in_=h_words[n][0].rearrange("p n t -> p (n t)").bitcast(I32),
                     )
-                if n + 1 < GATES:
-                    small_load(n + 1, q)
+                small_load(n + 1, q)
                 for j in range(CHUNK):
                     g = q * CHUNK + j
+                    start, slot = plane_of(g)
                     for part in range(parts):
                         cols = slice(part * width, (part + 1) * width)
                         nc.tensor.matmul_mx(
@@ -206,7 +214,7 @@ def tile_forcedgpulstmcell_k_kernel(
                             lhsT=x_codes[:, g * BATCH : (g + 1) * BATCH].bitcast(FP8X4),
                             lhsT_scale=x_planes[:, g * BATCH : (g + 1) * BATCH],
                             rhs=w[:, j, cols].bitcast(FP8X4),
-                            rhs_scale=planes[n][4 * j : P, q, cols],
+                            rhs_scale=planes[n][4 * start : P, slot, cols],
                             start=(g == 0),
                             stop=(g == PASSES - 1),
                         )

@@ -245,11 +245,11 @@ def tile_forcedgpulstmcell_k_kernel(
         nc.vector.tensor_mul(out=fresh[:], in0=i_gate[:], in1=g_gate[:])
         c_out = keep.tile([P, HIDDEN], F32, name="c_out")
         nc.vector.tensor_add(out=c_out[:], in0=kept[:], in1=fresh[:])
-        nc.scalar.dma_start(out=c_new, in_=c_out[:])
         tanh_c = keep.tile([P, HIDDEN], F32, name="tanh_c")
         nc.scalar.activation(out=tanh_c[:], in_=c_out[:], func=ACT.Tanh)
 
         halves = gate(3, ACT.Sigmoid, 2)
+        nc.sync.dma_start(out=c_new, in_=c_out[:])
         width = HIDDEN // 2
         for part, queue in ((0, nc.sync), (1, nc.scalar)):
             cols = slice(part * width, (part + 1) * width)

@@ -26,6 +26,7 @@ SLOTS = WHOLE + 2
 LAST = CHUNKS - 1
 WORDS_PASS = K_PASS // 2
 QUADRANT = 32
+LOAD = 2
 WEIGHT_BUFS = 12
 
 FLOPS = 2 * BATCH * (IN_FEATURES + HIDDEN) * 4 * HIDDEN
@@ -192,12 +193,13 @@ def tile_forcedgpulstmcell_k_kernel(
             for q in range(CHUNKS):
                 w = weights.tile([P, CHUNK, HIDDEN], U32, align_bytes=64, name="w")
                 from_x = min(CHUNK, X_PASSES - q * CHUNK)
-                nc.sync.dma_start(
-                    out=w[:, 0:from_x, :].bitcast(I32),
-                    in_=x_words[n][q * CHUNK : q * CHUNK + from_x]
-                    .rearrange("g p n t -> p g (n t)")
-                    .bitcast(I32),
-                )
+                for first in range(0, from_x, LOAD):
+                    g = q * CHUNK + first
+                    size = min(LOAD, from_x - first)
+                    nc.sync.dma_start(
+                        out=w[:, first : first + size, :].bitcast(I32),
+                        in_=x_words[n][g : g + size].rearrange("g p n t -> p g (n t)").bitcast(I32),
+                    )
                 if from_x < CHUNK:
                     nc.sync.dma_start(
                         out=w[:, from_x, :].bitcast(I32),

from contextlib import ExitStack

import concourse.mybir as mybir
from concourse.masks import make_identity

FP8X4 = mybir.dt.float8_e4m3fn_x4
BF16 = mybir.dt.bfloat16
F32 = mybir.dt.float32
I32 = mybir.dt.int32
U32 = mybir.dt.uint32
U8 = mybir.dt.uint8
ACT = mybir.ActivationFunctionType
ALU = mybir.AluOpType

P = 128
BATCH = 128
IN_FEATURES = 15872
HIDDEN = 512
K_PASS = 4 * P
X_PASSES = IN_FEATURES // K_PASS
PASSES = X_PASSES + HIDDEN // K_PASS
CHUNK = 4
CHUNKS = PASSES // CHUNK
WHOLE = X_PASSES // CHUNK
SLOTS = WHOLE + 2
LAST = CHUNKS - 1
WORDS_PASS = K_PASS // 2
QUADRANT = 32
LOAD = 2
WEIGHT_BUFS = 12

FLOPS = 2 * BATCH * (IN_FEATURES + HIDDEN) * 4 * HIDDEN


def scale_loads(planes, x_scales, h_scales):
    of_x = []
    of_h = []
    for r in range(4):
        for a in range(4):
            live = planes[QUADRANT * a : QUADRANT * a + 4 * CHUNK]
            of_x.append(
                (
                    live[r : 4 * CHUNK : 4, 0:WHOLE, :],
                    x_scales[0 : WHOLE * CHUNK, 4 * a + r, :].rearrange("(q j) n -> j q n", j=CHUNK),
                )
            )
    for a in range(4):
        live = planes[QUADRANT * a : QUADRANT * a + 4 * CHUNK]
        of_x.append((live[:, WHOLE, :], x_scales[X_PASSES - CHUNK : X_PASSES, 4 * a : 4 * a + 4, :]))
        of_h.append((live[0:4, WHOLE + 1, :], h_scales[0, 4 * a : 4 * a + 4, :]))
    return of_x, of_h


def plane_of(g):
    if g < WHOLE * CHUNK:
        return g % CHUNK, g // CHUNK
    if g < X_PASSES:
        return g - (X_PASSES - CHUNK), WHOLE
    return 0, WHOLE + 1


def tile_forcedgpulstmcell_k_kernel(
    tc,
    x,
    h,
    c,
    weight_ii_words,
    weight_ii_scales,
    weight_if_words,
    weight_if_scales,
    weight_ig_words,
    weight_ig_scales,
    weight_io_words,
    weight_io_scales,
    weight_hi_words,
    weight_hi_scales,
    weight_hf_words,
    weight_hf_scales,
    weight_hg_words,
    weight_hg_scales,
    weight_ho_words,
    weight_ho_scales,
    bias_i,
    bias_f,
    bias_g,
    bias_o,
    h_new,
    c_new,
):
    nc = tc.nc
    x_words = [weight_ii_words, weight_if_words, weight_ig_words, weight_io_words]
    x_scales = [weight_ii_scales, weight_if_scales, weight_ig_scales, weight_io_scales]
    h_words = [weight_hi_words, weight_hf_words, weight_hg_words, weight_ho_words]
    h_scales = [weight_hi_scales, weight_hf_scales, weight_hg_scales, weight_ho_scales]
    biases = [bias_i, bias_f, bias_g, bias_o]
    GATES = len(biases)

    with ExitStack() as stack:
        stack.enter_context(tc.manual_schedule())
        keep = stack.enter_context(tc.tile_pool(name="keep", bufs=1))
        raw_pool = stack.enter_context(tc.tile_pool(name="raw", bufs=CHUNKS // 2))
        stage = stack.enter_context(tc.tile_pool(name="stage", bufs=3))
        weights = stack.enter_context(tc.tile_pool(name="weights", bufs=WEIGHT_BUFS))
        psum_t = stack.enter_context(tc.psum_pool(name="psum_t", bufs=4))
        psum_bias = stack.enter_context(tc.psum_pool(name="psum_bias", bufs=1))
        psum_acc = stack.enter_context(tc.psum_pool(name="psum_acc", bufs=3))

        planes = []
        small_loads = []
        ident = keep.tile([P, P], F32, name="ident")
        make_identity(nc, ident[:])
        for n in range(GATES):
            gate_planes = keep.tile([P, SLOTS, HIDDEN], U8, align_bytes=64, name="planes%d" % n)
            nc.vector.memset(gate_planes[:].bitcast(I32), 0)
            planes.append(gate_planes)
            of_x, of_h = scale_loads(gate_planes, x_scales[n], h_scales[n])
            small_loads.append(of_h)
            for dst, src in of_x:
                nc.gpsimd.dma_start(out=dst.bitcast(F32), in_=src.bitcast(F32))

        def small_load(n, k):
            if n < GATES and k < len(small_loads[n]):
                dst, src = small_loads[n][k]
                nc.sync.dma_start(out=dst.bitcast(I32), in_=src.bitcast(I32))

        raws = []
        width = 2 * CHUNK * K_PASS
        for q in range(CHUNKS // 2):
            raw = raw_pool.tile([P, width], BF16, name="raw")
            first = q * width
            own = min(width, IN_FEATURES - first)
            nc.sync.dma_start(out=raw[:, :own], in_=x[:, first : first + own])
            if own < width:
                nc.sync.dma_start(out=raw[:, own:], in_=h)
            small_load(0, q)
            raws.append(raw)
        c_sb = keep.tile([P, HIDDEN], BF16, name="c_sb")
        nc.sync.dma_start(out=c_sb[:], in_=c)

        bias_rows = keep.tile([P, GATES * HIDDEN], BF16, name="bias_rows")
        nc.vector.memset(bias_rows[:], 0.0)
        ones = keep.tile([P, P], BF16, name="ones")
        nc.vector.memset(ones[:], 1.0)
        for n in range(GATES):
            nc.scalar.dma_start(
                out=bias_rows[0:1, n * HIDDEN : (n + 1) * HIDDEN],
                in_=biases[n].rearrange("(o n) -> o n", o=1),
            )

        x_codes = keep.tile([P, PASSES * BATCH], U32, align_bytes=64, name="x_codes")
        x_planes = keep.tile([P, PASSES * BATCH], U8, align_bytes=64, name="x_planes")
        for q in range(CHUNKS):
            half_raw = CHUNK * K_PASS * (q % 2)
            raw_words = raws[q // 2][:, half_raw : half_raw + CHUNK * K_PASS].bitcast(F32)
            grouped = stage.tile([P, CHUNK * K_PASS], BF16, align_bytes=64, name="grouped")
            grouped_words = grouped[:].bitcast(F32).rearrange("p (g b u) -> p g b u", g=CHUNK, u=2)
            for half in range(2):
                xt = psum_t.tile([P, 2, 2, BATCH], F32, name="xt")
                for g in range(2):
                    first = (2 * half + g) * WORDS_PASS
                    for u in range(2):
                        nc.tensor.transpose(
                            xt[:, g, u, :], raw_words[:, first + u : first + WORDS_PASS : 2], ident[:]
                        )
                side_by_side = xt[:].rearrange("p g u b -> p g b u")
                if half == 0:
                    nc.vector.tensor_copy(out=grouped_words[:, 0:2], in_=side_by_side)
                else:
                    nc.scalar.copy(out=grouped_words[:, 2:4], in_=side_by_side)
            cols = slice(q * CHUNK * BATCH, (q + 1) * CHUNK * BATCH)
            nc.vector.quantize_mx(
                out=x_codes[:, cols].bitcast(FP8X4), scales=x_planes[:, cols], in_=grouped[:]
            )

        bias_all = keep.tile([P, GATES, HIDDEN], F32, name="bias_all")
        for n in range(GATES):
            spread = psum_bias.tile([P, HIDDEN], F32, name="spread")
            nc.tensor.matmul(
                out=spread[:],
                lhsT=ones[:],
                rhs=bias_rows[:, n * HIDDEN : (n + 1) * HIDDEN],
                start=True,
                stop=True,
            )
            nc.scalar.copy(out=bias_all[:, n, :], in_=spread[:])

        def gate(n, func, parts):
            width = HIDDEN // parts
            accs = []
            for part in range(parts):
                acc = psum_acc.tile([P, HIDDEN], F32, name="acc")
                accs.append(acc)
            for q in range(CHUNKS):
                w = weights.tile([P, CHUNK, HIDDEN], U32, align_bytes=64, name="w")
                from_x = min(CHUNK, X_PASSES - q * CHUNK)
                for first in range(0, from_x, LOAD):
                    g = q * CHUNK + first
                    size = min(LOAD, from_x - first)
                    nc.sync.dma_start(
                        out=w[:, first : first + size, :].bitcast(I32),
                        in_=x_words[n][g : g + size].rearrange("g p n t -> p g (n t)").bitcast(I32),
                    )
                if from_x < CHUNK:
                    nc.sync.dma_start(
                        out=w[:, from_x, :].bitcast(I32),
                        in_=h_words[n][0].rearrange("p n t -> p (n t)").bitcast(I32),
                    )
                small_load(n + 1, q)
                for j in range(CHUNK):
                    g = q * CHUNK + j
                    start, slot = plane_of(g)
                    for part in range(parts):
                        cols = slice(part * width, (part + 1) * width)
                        nc.tensor.matmul_mx(
                            out=accs[part][:, 0:width],
                            lhsT=x_codes[:, g * BATCH : (g + 1) * BATCH].bitcast(FP8X4),
                            lhsT_scale=x_planes[:, g * BATCH : (g + 1) * BATCH],
                            rhs=w[:, j, cols].bitcast(FP8X4),
                            rhs_scale=planes[n][4 * start : P, slot, cols],
                            start=(g == 0),
                            stop=(g == PASSES - 1),
                        )
            biased = []
            for part in range(parts):
                total = stage.tile([P, HIDDEN], F32, name="total")
                nc.vector.tensor_tensor(
                    out=total[:, 0:width],
                    in0=accs[part][:, 0:width],
                    in1=bias_all[:, n, part * width : (part + 1) * width],
                    op=ALU.add,
                )
                biased.append(total)
            results = []
            for part in range(parts):
                result = keep.tile([P, width], F32, name="gate%d_%d" % (n, part))
                nc.scalar.activation(out=result[:], in_=biased[part][:, 0:width], func=func)
                results.append(result)
            return results

        (i_gate,) = gate(0, ACT.Sigmoid, 1)
        (f_gate,) = gate(1, ACT.Sigmoid, 1)
        kept = keep.tile([P, HIDDEN], F32, name="kept")
        nc.vector.tensor_mul(out=kept[:], in0=f_gate[:], in1=c_sb[:])

        (g_gate,) = gate(2, ACT.Tanh, 1)
        fresh = keep.tile([P, HIDDEN], F32, name="fresh")
        nc.vector.tensor_mul(out=fresh[:], in0=i_gate[:], in1=g_gate[:])
        c_out = keep.tile([P, HIDDEN], F32, name="c_out")
        nc.vector.tensor_add(out=c_out[:], in0=kept[:], in1=fresh[:])
        tanh_c = keep.tile([P, HIDDEN], F32, name="tanh_c")
        nc.scalar.activation(out=tanh_c[:], in_=c_out[:], func=ACT.Tanh)

        halves = gate(3, ACT.Sigmoid, 2)
        nc.sync.dma_start(out=c_new, in_=c_out[:])
        width = HIDDEN // 2
        for part, queue in ((0, nc.sync), (1, nc.scalar)):
            cols = slice(part * width, (part + 1) * width)
            h_out = keep.tile([P, width], F32, name="h_out%d" % part)
            nc.vector.tensor_mul(out=h_out[:], in0=halves[part][:], in1=tanh_c[:, cols])
            queue.dma_start(out=h_new[:, cols], in_=h_out[:])
